import numpy as np
import ml_dtypes


def mxq(x, axis, fmt="e4m3"):
    dtype, down = {"e4m3": (ml_dtypes.float8_e4m3fn, 7), "e5m2": (ml_dtypes.float8_e5m2, 14)}[fmt]
    v = np.moveaxis(np.asarray(x, np.float32).astype(ml_dtypes.bfloat16).astype(np.float64), axis, -1)
    blocks = v.reshape(v.shape[:-1] + (-1, 32))
    amax = np.abs(blocks).max(-1, keepdims=True)
    byte = np.maximum(np.where(amax > 0, np.frexp(amax)[1] - 1 + 127, 0) - down, 1)
    scale = np.exp2(byte - 127.0)
    codes = (blocks / scale).astype(np.float32).astype(dtype).astype(np.float64)
    return np.moveaxis((codes * scale).reshape(v.shape), -1, axis)


WIDE = False


def mx_kscale(k):
    if not WIDE:
        return np.ones(k)
    levels = np.array([10, -10, 5, -5, 0])
    a = np.random.permutation(np.resize(levels, k // 512 * 4)).reshape(k // 512, 4)
    idx = np.arange(k)
    return np.exp2(a[idx // 512, idx % 128 // 32])


BF16 = ml_dtypes.bfloat16


def bf(x):
    return np.asarray(x, np.float32).astype(BF16)


def f64(x):
    return np.asarray(x).astype(np.float64)


B, S, H, NH, NKV, HD = 4, 2048, 1024, 2, 1, 128
EPS = 1e-6


def rms_norm(x, w):
    var = np.mean(x * x, axis=-1, keepdims=True)
    return x * (1.0 / np.sqrt(var + EPS)) * w


def rotate_half(x):
    x1, x2 = np.split(x, 2, axis=-1)
    return np.concatenate([-x2, x1], axis=-1)


def setup_inputs():
    s = mx_kscale(H)
    inv_freq = 1.0 / (10000.0 ** (np.arange(0, HD, 2) / HD))
    freqs = np.arange(S)[:, None] * inv_freq[None, :]
    emb = np.concatenate([freqs, freqs], axis=-1)
    return {"hidden_states": bf(np.random.standard_normal((B, S, H)) * s),
            "cos": bf(np.cos(emb)),
            "sin": bf(np.sin(emb)),
            "wq": bf(np.random.standard_normal((NH * HD, H)) / np.sqrt(H) / s[None, :]),
            "wk": bf(np.random.standard_normal((NKV * HD, H)) / np.sqrt(H) / s[None, :]),
            "q_norm_w": bf(1.0 + 0.1 * np.random.standard_normal(HD)),
            "k_norm_w": bf(1.0 + 0.1 * np.random.standard_normal(HD)),
            "ssmax_scale": bf((1.0 + 0.2 * np.random.standard_normal((1, NH, 1, 1))) / np.log(S))}


def reference(hidden_states, cos, sin, wq, wk, q_norm_w, k_norm_w, ssmax_scale):
    xq = mxq(f64(hidden_states), 2, "e4m3")
    q = (xq @ mxq(f64(wq), 1, "e4m3").T).reshape(B, S, NH, HD)
    k = (xq @ mxq(f64(wk), 1, "e4m3").T).reshape(B, S, NKV, HD)
    q = rms_norm(q, f64(q_norm_w)).transpose(0, 2, 1, 3)
    k = rms_norm(k, f64(k_norm_w)).transpose(0, 2, 1, 3)
    c = f64(cos)[None, None]
    sn = f64(sin)[None, None]
    q = q * c + rotate_half(q) * sn
    k = k * c + rotate_half(k) * sn
    q = q * (f64(ssmax_scale) * np.log(S))
    return q, k

@@ -1,0 +1,230 @@
+import math
+from contextlib import ExitStack
+
+import concourse.mybir as mybir
+from concourse.masks import make_identity
+
+F32 = mybir.dt.float32
+BF16 = mybir.dt.bfloat16
+U32 = mybir.dt.uint32
+U8 = mybir.dt.uint8
+FP8X4 = mybir.dt.float8_e4m3fn_x4
+ALU = mybir.AluOpType
+ACT = mybir.ActivationFunctionType
+
+P = 128
+BATCH = 4
+SEQ = 2048
+HIDDEN = 1024
+Q_HEADS = 2
+HEADS = 3
+HD = 128
+HALF = HD // 2
+EPS = 1e-6
+
+K_PASS = 4 * P
+PASSES = HIDDEN // K_PASS
+WORDS = HIDDEN // 2
+BLOCKS = WORDS // P
+SLICES = SEQ // P
+GROUP = 4
+UNIT = 2
+
+FLOPS = 2 * BATCH * SEQ * HIDDEN * HEADS * HD
+
+
+def transpose_rows(nc, psum_t, ident, words):
+    bank = psum_t.tile([P, WORDS], F32, name="bank")
+    for j in range(BLOCKS):
+        cols = slice(j * P, (j + 1) * P)
+        nc.tensor.transpose(bank[:, cols], words[:, cols], ident[:])
+    return bank
+
+
+def copy_grouped(nc, bank, grouped_words):
+    nc.scalar.copy(
+        out=grouped_words,
+        in_=bank[:].rearrange("p (g u r) -> p g r u", g=PASSES, u=2),
+    )
+
+
+def tile_biboattention_pa_t_kernel(
+    tc, hidden_states, cos, sin, wq, wk, q_norm_w, k_norm_w, ssmax_scale, out_0, out_1
+):
+    nc = tc.nc
+    with ExitStack() as ctx:
+        const = ctx.enter_context(tc.tile_pool(name="const", bufs=1))
+        x_pool = ctx.enter_context(tc.tile_pool(name="x", bufs=6))
+        angle_pool = ctx.enter_context(tc.tile_pool(name="angle", bufs=2))
+        table_pool = ctx.enter_context(tc.tile_pool(name="table", bufs=2))
+        mx_pool = ctx.enter_context(tc.tile_pool(name="mx", bufs=3))
+        stat_pool = ctx.enter_context(tc.tile_pool(name="stat", bufs=4))
+        prod_pool = ctx.enter_context(tc.tile_pool(name="prod", bufs=3))
+        out_pool = ctx.enter_context(tc.tile_pool(name="out", bufs=3))
+        psum_t = ctx.enter_context(tc.psum_pool(name="psum_t", bufs=4))
+        psum_o = ctx.enter_context(tc.psum_pool(name="psum_o", bufs=4))
+
+        ident = const.tile([P, P], F32)
+        make_identity(nc, ident[:])
+        eps = const.tile([P, 1], F32)
+        nc.vector.memset(eps[:], EPS)
+        warm = const.tile([P, 1], F32)
+        nc.scalar.activation(out=warm[:], in_=eps[:], func=ACT.Sqrt)
+
+        w_raw = const.tile([P, HEADS, HIDDEN], BF16)
+        nc.sync.dma_start(out=w_raw[:, 0:Q_HEADS, :], in_=wq.rearrange("(a p) k -> p a k", p=P))
+        nc.sync.dma_start(out=w_raw[:, Q_HEADS, :], in_=wk)
+        wq_grouped = const.tile([P, PASSES * Q_HEADS * HD * 4], BF16, align_bytes=64)
+        wk_grouped = const.tile([P, PASSES * HD * 4], BF16, align_bytes=64)
+        wq_words = wq_grouped[:].bitcast(F32).rearrange("p (g n u) -> p g n u", g=PASSES, u=2)
+        wk_words = wk_grouped[:].bitcast(F32).rearrange("p (g n u) -> p g n u", g=PASSES, u=2)
+        for h in range(HEADS):
+            bank = transpose_rows(nc, psum_t, ident, w_raw[:, h, :].bitcast(F32))
+            if h < Q_HEADS:
+                copy_grouped(nc, bank, wq_words[:, :, h * HD : (h + 1) * HD, :])
+            else:
+                copy_grouped(nc, bank, wk_words)
+        wq_codes = const.tile([P, PASSES * Q_HEADS * HD], U32, align_bytes=64)
+        wq_scales = const.tile([P, PASSES * Q_HEADS * HD], U8, align_bytes=64)
+        wk_codes = const.tile([P, PASSES * HD], U32, align_bytes=64)
+        wk_scales = const.tile([P, PASSES * HD], U8, align_bytes=64)
+        nc.vector.quantize_mx(out=wq_codes[:].bitcast(FP8X4), scales=wq_scales[:], in_=wq_grouped[:])
+        nc.vector.quantize_mx(out=wk_codes[:].bitcast(FP8X4), scales=wk_scales[:], in_=wk_grouped[:])
+        projections = (
+            (slice(0, Q_HEADS * HD), wq_codes, wq_scales, Q_HEADS * HD),
+            (slice(Q_HEADS * HD, HEADS * HD), wk_codes, wk_scales, HD),
+        )
+
+        wq_rows = const.tile([P, HD], BF16)
+        wk_rows = const.tile([P, HD], BF16)
+        gain_rows = const.tile([P, Q_HEADS], BF16)
+        nc.scalar.dma_start(out=wq_rows[:], in_=q_norm_w.partition_broadcast(P))
+        nc.scalar.dma_start(out=wk_rows[:], in_=k_norm_w.partition_broadcast(P))
+        nc.scalar.dma_start(
+            out=gain_rows[:], in_=ssmax_scale.rearrange("a h b c -> (a h b c)").partition_broadcast(P)
+        )
+        gain = const.tile([P, Q_HEADS], F32)
+        nc.vector.tensor_scalar_mul(out=gain[:], in0=gain_rows[:], scalar1=math.log(SEQ))
+        w_cos = const.tile([P, HEADS, HD], F32)
+        for h in range(Q_HEADS):
+            nc.vector.tensor_scalar_mul(out=w_cos[:, h, :], in0=wq_rows[:], scalar1=gain[:, h : h + 1])
+        nc.vector.tensor_copy(out=w_cos[:, Q_HEADS, :], in_=wk_rows[:])
+        w_sin = const.tile([P, HEADS, HD], F32)
+        nc.vector.tensor_copy(out=w_sin[:, :, 0:HALF], in_=w_cos[:, :, 0:HALF])
+        nc.vector.tensor_scalar_mul(out=w_sin[:, :, HALF:HD], in0=w_cos[:, :, HALF:HD], scalar1=-1.0)
+
+        cos_slices = cos.rearrange("(p t) d -> p t d", t=SLICES)
+        sin_slices = sin.rearrange("(p t) d -> p t d", t=SLICES)
+
+        for c in range(SLICES // GROUP):
+            group_slices = slice(c * GROUP, (c + 1) * GROUP)
+
+            angle = angle_pool.tile([P, 2, GROUP, HD], BF16)
+            nc.sync.dma_start(out=angle[:, 0], in_=cos_slices[:, group_slices, :])
+            nc.sync.dma_start(out=angle[:, 1], in_=sin_slices[:, group_slices, :])
+            table = table_pool.tile([P, GROUP, HEADS, 2, HD], F32)
+            engine = nc.vector if c == 0 else nc.gpsimd
+            engine.tensor_tensor(
+                out=table[:, :, :, 0, :],
+                in0=angle[:, 0].unsqueeze(2).to_broadcast([P, GROUP, HEADS, HD]),
+                in1=w_cos[:].unsqueeze(1).to_broadcast([P, GROUP, HEADS, HD]),
+                op=ALU.mult,
+            )
+            for i in range(2):
+                here = slice(i * HALF, (i + 1) * HALF)
+                there = slice((1 - i) * HALF, (2 - i) * HALF)
+                engine.tensor_tensor(
+                    out=table[:, :, :, 1, here],
+                    in0=angle[:, 1, :, there].unsqueeze(2).to_broadcast([P, GROUP, HEADS, HALF]),
+                    in1=w_sin[:, :, here].unsqueeze(1).to_broadcast([P, GROUP, HEADS, HALF]),
+                    op=ALU.mult,
+                )
+
+            for b in range(BATCH):
+                x_rows = x_pool.tile([P, GROUP * HIDDEN], BF16)
+                nc.sync.dma_start(
+                    out=x_rows[:].rearrange("p (t k) -> p t k", t=GROUP),
+                    in_=hidden_states[b].rearrange("(p t) k -> p t k", t=SLICES)[:, group_slices, :],
+                )
+                x_words = x_rows[:].bitcast(F32)
+                result = out_pool.tile([P, HEADS, GROUP, HD], F32)
+
+                for v in range(GROUP // UNIT):
+                    grouped = mx_pool.tile([P, UNIT * HIDDEN], BF16, align_bytes=64)
+                    grouped_words = grouped[:].bitcast(F32).rearrange(
+                        "p (s g r u) -> p s g r u", s=UNIT, g=PASSES, u=2
+                    )
+                    banks = []
+                    for s in range(UNIT):
+                        t = v * UNIT + s
+                        banks.append(
+                            transpose_rows(nc, psum_t, ident, x_words[:, t * WORDS : (t + 1) * WORDS])
+                        )
+                    for s in range(UNIT):
+                        copy_grouped(nc, banks[s], grouped_words[:, s])
+                    codes = mx_pool.tile([P, UNIT * PASSES * P], U32, align_bytes=64)
+                    scales = mx_pool.tile([P, UNIT * PASSES * P], U8, align_bytes=64)
+                    nc.vector.quantize_mx(out=codes[:].bitcast(FP8X4), scales=scales[:], in_=grouped[:])
+
+                    raws = []
+                    sumsq = stat_pool.tile([P, UNIT * HEADS], F32)
+                    for s in range(UNIT):
+                        raw = psum_o.tile([P, HEADS * HD], F32, name="raw")
+                        for cols, w_codes, w_scales, width in projections:
+                            for g in range(PASSES):
+                                tokens = slice((s * PASSES + g) * P, (s * PASSES + g + 1) * P)
+                                features = slice(g * width, (g + 1) * width)
+                                nc.tensor.matmul_mx(
+                                    out=raw[:, cols],
+                                    lhsT=codes[:, tokens].bitcast(FP8X4),
+                                    lhsT_scale=scales[:, tokens],
+                                    rhs=w_codes[:, features].bitcast(FP8X4),
+                                    rhs_scale=w_scales[:, features],
+                                    start=(g == 0),
+                                    stop=(g == PASSES - 1),
+                                )
+                        raws.append(raw)
+                    for s in range(UNIT):
+                        squares = stat_pool.tile([P, HEADS * HD], BF16)
+                        for h in range(HEADS):
+                            head = slice(h * HD, (h + 1) * HD)
+                            nc.scalar.activation(
+                                out=squares[:, head],
+                                in_=raws[s][:, head],
+                                func=ACT.Square,
+                                accum_out=sumsq[:, s * HEADS + h : s * HEADS + h + 1],
+                            )
+                    rms = stat_pool.tile([P, UNIT * HEADS], F32)
+                    nc.scalar.activation(out=rms[:], in_=sumsq[:], func=ACT.Sqrt, bias=eps[:], scale=1.0 / HD)
+                    rstd = stat_pool.tile([P, UNIT * HEADS], F32)
+                    nc.vector.reciprocal(out=rstd[:], in_=rms[:])
+
+                    products = prod_pool.tile([P, HEADS, UNIT, 2, HD], F32)
+                    for s in range(UNIT):
+                        for h in range(HEADS):
+                            nc.vector.scalar_tensor_tensor(
+                                out=products[:, h, s],
+                                in0=raws[s][:, h * HD : (h + 1) * HD].unsqueeze(1).to_broadcast([P, 2, HD]),
+                                scalar=rstd[:, s * HEADS + h : s * HEADS + h + 1],
+                                in1=table[:, v * UNIT + s, h],
+                                op0=ALU.mult,
+                                op1=ALU.mult,
+                            )
+                    for i in range(2):
+                        here = slice(i * HALF, (i + 1) * HALF)
+                        there = slice((1 - i) * HALF, (2 - i) * HALF)
+                        nc.gpsimd.tensor_tensor(
+                            out=result[:, :, v * UNIT : (v + 1) * UNIT, here],
+                            in0=products[:, :, :, 0, here],
+                            in1=products[:, :, :, 1, there],
+                            op=ALU.add,
+                        )
+
+                nc.sync.dma_start(
+                    out=out_0[b].rearrange("h (p t) d -> p h t d", t=SLICES)[:, :, group_slices, :],
+                    in_=result[:, 0:Q_HEADS],
+                )
+                nc.sync.dma_start(
+                    out=out_1[b, 0].rearrange("(p t) d -> p t d", t=SLICES)[:, group_slices, :],
+                    in_=result[:, Q_HEADS],
+                )

@@ -29,6 +29,12 @@ BLOCKS = WORDS // P
 SLICES = SEQ // P
 GROUP = 4
 UNIT = 2
+CHUNKS = SLICES // GROUP
+GROUPS = CHUNKS * BATCH
+UNITS_PER_GROUP = GROUP // UNIT
+UNITS_PER_CHUNK = BATCH * UNITS_PER_GROUP
+UNITS = GROUPS * UNITS_PER_GROUP
+LOAD_AHEAD = 5
 
 FLOPS = 2 * BATCH * SEQ * HIDDEN * HEADS * HD
 
@@ -54,26 +60,207 @@ def tile_biboattention_pa_t_kernel(
     nc = tc.nc
     with ExitStack() as ctx:
         const = ctx.enter_context(tc.tile_pool(name="const", bufs=1))
-        x_pool = ctx.enter_context(tc.tile_pool(name="x", bufs=6))
+        x_pool = ctx.enter_context(tc.tile_pool(name="x", bufs=LOAD_AHEAD + 1))
         angle_pool = ctx.enter_context(tc.tile_pool(name="angle", bufs=2))
         table_pool = ctx.enter_context(tc.tile_pool(name="table", bufs=2))
         mx_pool = ctx.enter_context(tc.tile_pool(name="mx", bufs=3))
         stat_pool = ctx.enter_context(tc.tile_pool(name="stat", bufs=4))
         prod_pool = ctx.enter_context(tc.tile_pool(name="prod", bufs=3))
         out_pool = ctx.enter_context(tc.tile_pool(name="out", bufs=3))
-        psum_t = ctx.enter_context(tc.psum_pool(name="psum_t", bufs=4))
-        psum_o = ctx.enter_context(tc.psum_pool(name="psum_o", bufs=4))
+        psum_t = ctx.enter_context(tc.psum_pool(name="psum_t", bufs=2 * UNIT))
+        psum_o = ctx.enter_context(tc.psum_pool(name="psum_o", bufs=2 * UNIT))
+        ctx.enter_context(tc.manual_schedule())
+
+        cos_slices = cos.rearrange("(p t) d -> p t d", t=SLICES)
+        sin_slices = sin.rearrange("(p t) d -> p t d", t=SLICES)
+
+        angles = {}
+        tables = {}
+        x_words = {}
+        banks = {}
+        groupeds = {}
+        operands = {}
+        raws = {}
+        rstds = {}
+        products = {}
+        results = {}
+
+        def group_slices(n):
+            chunk = n // BATCH
+            return slice(chunk * GROUP, (chunk + 1) * GROUP)
+
+        def load_angles(chunk):
+            angle = angle_pool.tile([P, 2, GROUP, HD], BF16)
+            nc.sync.dma_start(out=angle[:, 0], in_=cos_slices[:, group_slices(chunk * BATCH), :])
+            nc.sync.dma_start(out=angle[:, 1], in_=sin_slices[:, group_slices(chunk * BATCH), :])
+            angles[chunk] = angle
+
+        def build_tables(chunk, v):
+            if v == 0:
+                tables[chunk] = table_pool.tile([P, GROUP, HEADS, 2, HD], F32, name="table")
+            table = tables[chunk]
+            angle = angles[chunk]
+            mine = slice(v * UNIT, (v + 1) * UNIT)
+            nc.vector.tensor_tensor(
+                out=table[:, mine, :, 0, :],
+                in0=angle[:, 0, mine].unsqueeze(2).to_broadcast([P, UNIT, HEADS, HD]),
+                in1=w_cos[:].unsqueeze(1).to_broadcast([P, UNIT, HEADS, HD]),
+                op=ALU.mult,
+            )
+            for i in range(2):
+                here = slice(i * HALF, (i + 1) * HALF)
+                there = slice((1 - i) * HALF, (2 - i) * HALF)
+                nc.vector.tensor_tensor(
+                    out=table[:, mine, :, 1, here],
+                    in0=angle[:, 1, mine, there].unsqueeze(2).to_broadcast([P, UNIT, HEADS, HALF]),
+                    in1=w_sin[:, :, here].unsqueeze(1).to_broadcast([P, UNIT, HEADS, HALF]),
+                    op=ALU.mult,
+                )
+
+        def load_rows(n):
+            x_rows = x_pool.tile([P, GROUP * HIDDEN], BF16)
+            nc.sync.dma_start(
+                out=x_rows[:].rearrange("p (t k) -> p t k", t=GROUP),
+                in_=hidden_states[n % BATCH].rearrange("(p t) k -> p t k", t=SLICES)[:, group_slices(n), :],
+            )
+            x_words[n] = x_rows[:].bitcast(F32)
+
+        def transpose_unit(u):
+            words = x_words[u // UNITS_PER_GROUP]
+            first = (u % UNITS_PER_GROUP) * UNIT
+            banks[u] = [
+                transpose_rows(nc, psum_t, ident, words[:, t * WORDS : (t + 1) * WORDS])
+                for t in range(first, first + UNIT)
+            ]
+
+        def copy_unit(u):
+            grouped = mx_pool.tile([P, UNIT * HIDDEN], BF16, align_bytes=64)
+            grouped_words = grouped[:].bitcast(F32).rearrange(
+                "p (s g r u) -> p s g r u", s=UNIT, g=PASSES, u=2
+            )
+            for s in range(UNIT):
+                copy_grouped(nc, banks[u][s], grouped_words[:, s])
+            groupeds[u] = grouped
+
+        def quantise_unit(u):
+            codes = mx_pool.tile([P, UNIT * PASSES * P], U32, align_bytes=64)
+            scales = mx_pool.tile([P, UNIT * PASSES * P], U8, align_bytes=64)
+            nc.vector.quantize_mx(out=codes[:].bitcast(FP8X4), scales=scales[:], in_=groupeds[u][:])
+            operands[u] = (codes, scales)
+
+        def project_unit(u):
+            codes, scales = operands[u]
+            raws[u] = []
+            for s in range(UNIT):
+                raw = psum_o.tile([P, HEADS * HD], F32)
+                for cols, w_codes, w_scales, width in projections:
+                    for g in range(PASSES):
+                        tokens = slice((s * PASSES + g) * P, (s * PASSES + g + 1) * P)
+                        features = slice(g * width, (g + 1) * width)
+                        nc.tensor.matmul_mx(
+                            out=raw[:, cols],
+                            lhsT=codes[:, tokens].bitcast(FP8X4),
+                            lhsT_scale=scales[:, tokens],
+                            rhs=w_codes[:, features].bitcast(FP8X4),
+                            rhs_scale=w_scales[:, features],
+                            start=(g == 0),
+                            stop=(g == PASSES - 1),
+                        )
+                raws[u].append(raw)
+
+        def norm_unit(u):
+            sumsq = stat_pool.tile([P, UNIT * HEADS], F32)
+            for s in range(UNIT):
+                squares = stat_pool.tile([P, HEADS * HD], BF16)
+                for h in range(HEADS):
+                    head = slice(h * HD, (h + 1) * HD)
+                    nc.scalar.activation(
+                        out=squares[:, head],
+                        in_=raws[u][s][:, head],
+                        func=ACT.Square,
+                        accum_out=sumsq[:, s * HEADS + h : s * HEADS + h + 1],
+                    )
+            rstd = stat_pool.tile([P, UNIT * HEADS], F32)
+            nc.scalar.activation(
+                out=rstd[:], in_=sumsq[:], func=ACT.Abs_reciprocal_sqrt, bias=eps[:], scale=1.0 / HD
+            )
+            rstds[u] = rstd
+
+        def rotate_unit(u):
+            table = tables[u // UNITS_PER_CHUNK]
+            first = (u % UNITS_PER_GROUP) * UNIT
+            product = prod_pool.tile([P, HEADS, UNIT, 2, HD], F32)
+            for s in range(UNIT):
+                for h in range(HEADS):
+                    nc.vector.scalar_tensor_tensor(
+                        out=product[:, h, s],
+                        in0=raws[u][s][:, h * HD : (h + 1) * HD].unsqueeze(1).to_broadcast([P, 2, HD]),
+                        scalar=rstds[u][:, s * HEADS + h : s * HEADS + h + 1],
+                        in1=table[:, first + s, h],
+                        op0=ALU.mult,
+                        op1=ALU.mult,
+                    )
+            products[u] = product
+
+        def add_unit(u):
+            n = u // UNITS_PER_GROUP
+            first = (u % UNITS_PER_GROUP) * UNIT
+            if first == 0:
+                results[n] = out_pool.tile([P, HEADS, GROUP, HD], F32, name="result")
+            for i in range(2):
+                here = slice(i * HALF, (i + 1) * HALF)
+                there = slice((1 - i) * HALF, (2 - i) * HALF)
+                nc.gpsimd.tensor_tensor(
+                    out=results[n][:, :, first : first + UNIT, here],
+                    in0=products[u][:, :, :, 0, here],
+                    in1=products[u][:, :, :, 1, there],
+                    op=ALU.add,
+                )
+
+        def store_group(n):
+            b = n % BATCH
+            nc.sync.dma_start(
+                out=out_0[b].rearrange("h (p t) d -> p h t d", t=SLICES)[:, :, group_slices(n), :],
+                in_=results[n][:, 0:Q_HEADS],
+            )
+            nc.sync.dma_start(
+                out=out_1[b, 0].rearrange("(p t) d -> p t d", t=SLICES)[:, group_slices(n), :],
+                in_=results[n][:, Q_HEADS],
+            )
+
+        wq_rows = const.tile([P, HD], BF16)
+        wk_rows = const.tile([P, HD], BF16)
+        gain_rows = const.tile([P, Q_HEADS], BF16)
+        nc.scalar.dma_start(out=wq_rows[:], in_=q_norm_w.partition_broadcast(P))
+        nc.scalar.dma_start(out=wk_rows[:], in_=k_norm_w.partition_broadcast(P))
+        nc.scalar.dma_start(
+            out=gain_rows[:], in_=ssmax_scale.rearrange("a h b c -> (a h b c)").partition_broadcast(P)
+        )
+        w_raw = const.tile([P, HEADS, HIDDEN], BF16)
+        nc.sync.dma_start(out=w_raw[:, 0:Q_HEADS, :], in_=wq.rearrange("(a p) k -> p a k", p=P))
+        nc.sync.dma_start(out=w_raw[:, Q_HEADS, :], in_=wk)
+        load_angles(0)
+        for n in range(LOAD_AHEAD):
+            load_rows(n)
 
         ident = const.tile([P, P], F32)
         make_identity(nc, ident[:])
         eps = const.tile([P, 1], F32)
         nc.vector.memset(eps[:], EPS)
         warm = const.tile([P, 1], F32)
-        nc.scalar.activation(out=warm[:], in_=eps[:], func=ACT.Sqrt)
+        nc.scalar.activation(out=warm[:], in_=eps[:], func=ACT.Abs_reciprocal_sqrt)
 
-        w_raw = const.tile([P, HEADS, HIDDEN], BF16)
-        nc.sync.dma_start(out=w_raw[:, 0:Q_HEADS, :], in_=wq.rearrange("(a p) k -> p a k", p=P))
-        nc.sync.dma_start(out=w_raw[:, Q_HEADS, :], in_=wk)
+        gain = const.tile([P, Q_HEADS], F32)
+        nc.vector.tensor_scalar_mul(out=gain[:], in0=gain_rows[:], scalar1=math.log(SEQ))
+        w_cos = const.tile([P, HEADS, HD], F32)
+        for h in range(Q_HEADS):
+            nc.vector.tensor_scalar_mul(out=w_cos[:, h, :], in0=wq_rows[:], scalar1=gain[:, h : h + 1])
+        nc.vector.tensor_copy(out=w_cos[:, Q_HEADS, :], in_=wk_rows[:])
+        w_sin = const.tile([P, HEADS, HD], F32)
+        nc.vector.tensor_copy(out=w_sin[:, :, 0:HALF], in_=w_cos[:, :, 0:HALF])
+        nc.vector.tensor_scalar_mul(out=w_sin[:, :, HALF:HD], in0=w_cos[:, :, HALF:HD], scalar1=-1.0)
+        build_tables(0, 0)
+
         wq_grouped = const.tile([P, PASSES * Q_HEADS * HD * 4], BF16, align_bytes=64)
         wk_grouped = const.tile([P, PASSES * HD * 4], BF16, align_bytes=64)
         wq_words = wq_grouped[:].bitcast(F32).rearrange("p (g n u) -> p g n u", g=PASSES, u=2)
@@ -95,136 +282,23 @@ def tile_biboattention_pa_t_kernel(
             (slice(Q_HEADS * HD, HEADS * HD), wk_codes, wk_scales, HD),
         )
 
-        wq_rows = const.tile([P, HD], BF16)
-        wk_rows = const.tile([P, HD], BF16)
-        gain_rows = const.tile([P, Q_HEADS], BF16)
-        nc.scalar.dma_start(out=wq_rows[:], in_=q_norm_w.partition_broadcast(P))
-        nc.scalar.dma_start(out=wk_rows[:], in_=k_norm_w.partition_broadcast(P))
-        nc.scalar.dma_start(
-            out=gain_rows[:], in_=ssmax_scale.rearrange("a h b c -> (a h b c)").partition_broadcast(P)
-        )
-        gain = const.tile([P, Q_HEADS], F32)
-        nc.vector.tensor_scalar_mul(out=gain[:], in0=gain_rows[:], scalar1=math.log(SEQ))
-        w_cos = const.tile([P, HEADS, HD], F32)
-        for h in range(Q_HEADS):
-            nc.vector.tensor_scalar_mul(out=w_cos[:, h, :], in0=wq_rows[:], scalar1=gain[:, h : h + 1])
-        nc.vector.tensor_copy(out=w_cos[:, Q_HEADS, :], in_=wk_rows[:])
-        w_sin = const.tile([P, HEADS, HD], F32)
-        nc.vector.tensor_copy(out=w_sin[:, :, 0:HALF], in_=w_cos[:, :, 0:HALF])
-        nc.vector.tensor_scalar_mul(out=w_sin[:, :, HALF:HD], in0=w_cos[:, :, HALF:HD], scalar1=-1.0)
-
-        cos_slices = cos.rearrange("(p t) d -> p t d", t=SLICES)
-        sin_slices = sin.rearrange("(p t) d -> p t d", t=SLICES)
-
-        for c in range(SLICES // GROUP):
-            group_slices = slice(c * GROUP, (c + 1) * GROUP)
-
-            angle = angle_pool.tile([P, 2, GROUP, HD], BF16)
-            nc.sync.dma_start(out=angle[:, 0], in_=cos_slices[:, group_slices, :])
-            nc.sync.dma_start(out=angle[:, 1], in_=sin_slices[:, group_slices, :])
-            table = table_pool.tile([P, GROUP, HEADS, 2, HD], F32)
-            engine = nc.vector if c == 0 else nc.gpsimd
-            engine.tensor_tensor(
-                out=table[:, :, :, 0, :],
-                in0=angle[:, 0].unsqueeze(2).to_broadcast([P, GROUP, HEADS, HD]),
-                in1=w_cos[:].unsqueeze(1).to_broadcast([P, GROUP, HEADS, HD]),
-                op=ALU.mult,
-            )
-            for i in range(2):
-                here = slice(i * HALF, (i + 1) * HALF)
-                there = slice((1 - i) * HALF, (2 - i) * HALF)
-                engine.tensor_tensor(
-                    out=table[:, :, :, 1, here],
-                    in0=angle[:, 1, :, there].unsqueeze(2).to_broadcast([P, GROUP, HEADS, HALF]),
-                    in1=w_sin[:, :, here].unsqueeze(1).to_broadcast([P, GROUP, HEADS, HALF]),
-                    op=ALU.mult,
-                )
-
-            for b in range(BATCH):
-                x_rows = x_pool.tile([P, GROUP * HIDDEN], BF16)
-                nc.sync.dma_start(
-                    out=x_rows[:].rearrange("p (t k) -> p t k", t=GROUP),
-                    in_=hidden_states[b].rearrange("(p t) k -> p t k", t=SLICES)[:, group_slices, :],
-                )
-                x_words = x_rows[:].bitcast(F32)
-                result = out_pool.tile([P, HEADS, GROUP, HD], F32)
-
-                for v in range(GROUP // UNIT):
-                    grouped = mx_pool.tile([P, UNIT * HIDDEN], BF16, align_bytes=64)
-                    grouped_words = grouped[:].bitcast(F32).rearrange(
-                        "p (s g r u) -> p s g r u", s=UNIT, g=PASSES, u=2
-                    )
-                    banks = []
-                    for s in range(UNIT):
-                        t = v * UNIT + s
-                        banks.append(
-                            transpose_rows(nc, psum_t, ident, x_words[:, t * WORDS : (t + 1) * WORDS])
-                        )
-                    for s in range(UNIT):
-                        copy_grouped(nc, banks[s], grouped_words[:, s])
-                    codes = mx_pool.tile([P, UNIT * PASSES * P], U32, align_bytes=64)
-                    scales = mx_pool.tile([P, UNIT * PASSES * P], U8, align_bytes=64)
-                    nc.vector.quantize_mx(out=codes[:].bitcast(FP8X4), scales=scales[:], in_=grouped[:])
-
-                    raws = []
-                    sumsq = stat_pool.tile([P, UNIT * HEADS], F32)
-                    for s in range(UNIT):
-                        raw = psum_o.tile([P, HEADS * HD], F32, name="raw")
-                        for cols, w_codes, w_scales, width in projections:
-                            for g in range(PASSES):
-                                tokens = slice((s * PASSES + g) * P, (s * PASSES + g + 1) * P)
-                                features = slice(g * width, (g + 1) * width)
-                                nc.tensor.matmul_mx(
-                                    out=raw[:, cols],
-                                    lhsT=codes[:, tokens].bitcast(FP8X4),
-                                    lhsT_scale=scales[:, tokens],
-                                    rhs=w_codes[:, features].bitcast(FP8X4),
-                                    rhs_scale=w_scales[:, features],
-                                    start=(g == 0),
-                                    stop=(g == PASSES - 1),
-                                )
-                        raws.append(raw)
-                    for s in range(UNIT):
-                        squares = stat_pool.tile([P, HEADS * HD], BF16)
-                        for h in range(HEADS):
-                            head = slice(h * HD, (h + 1) * HD)
-                            nc.scalar.activation(
-                                out=squares[:, head],
-                                in_=raws[s][:, head],
-                                func=ACT.Square,
-                                accum_out=sumsq[:, s * HEADS + h : s * HEADS + h + 1],
-                            )
-                    rms = stat_pool.tile([P, UNIT * HEADS], F32)
-                    nc.scalar.activation(out=rms[:], in_=sumsq[:], func=ACT.Sqrt, bias=eps[:], scale=1.0 / HD)
-                    rstd = stat_pool.tile([P, UNIT * HEADS], F32)
-                    nc.vector.reciprocal(out=rstd[:], in_=rms[:])
-
-                    products = prod_pool.tile([P, HEADS, UNIT, 2, HD], F32)
-                    for s in range(UNIT):
-                        for h in range(HEADS):
-                            nc.vector.scalar_tensor_tensor(
-                                out=products[:, h, s],
-                                in0=raws[s][:, h * HD : (h + 1) * HD].unsqueeze(1).to_broadcast([P, 2, HD]),
-                                scalar=rstd[:, s * HEADS + h : s * HEADS + h + 1],
-                                in1=table[:, v * UNIT + s, h],
-                                op0=ALU.mult,
-                                op1=ALU.mult,
-                            )
-                    for i in range(2):
-                        here = slice(i * HALF, (i + 1) * HALF)
-                        there = slice((1 - i) * HALF, (2 - i) * HALF)
-                        nc.gpsimd.tensor_tensor(
-                            out=result[:, :, v * UNIT : (v + 1) * UNIT, here],
-                            in0=products[:, :, :, 0, here],
-                            in1=products[:, :, :, 1, there],
-                            op=ALU.add,
-                        )
-
-                nc.sync.dma_start(
-                    out=out_0[b].rearrange("h (p t) d -> p h t d", t=SLICES)[:, :, group_slices, :],
-                    in_=result[:, 0:Q_HEADS],
-                )
-                nc.sync.dma_start(
-                    out=out_1[b, 0].rearrange("(p t) d -> p t d", t=SLICES)[:, group_slices, :],
-                    in_=result[:, Q_HEADS],
-                )
+        for step in range(UNITS + 1):
+            if step % UNITS_PER_GROUP == 0 and step // UNITS_PER_GROUP + LOAD_AHEAD < GROUPS:
+                load_rows(step // UNITS_PER_GROUP + LOAD_AHEAD)
+            if step % UNITS_PER_CHUNK == 0 and step // UNITS_PER_CHUNK + 1 < CHUNKS:
+                load_angles(step // UNITS_PER_CHUNK + 1)
+            if step < UNITS:
+                transpose_unit(step)
+                copy_unit(step)
+                quantise_unit(step)
+            following = step + 1
+            if following < UNITS and following % UNITS_PER_CHUNK < UNITS_PER_GROUP:
+                build_tables(following // UNITS_PER_CHUNK, following % UNITS_PER_CHUNK)
+            if step >= 1:
+                done = step - 1
+                project_unit(done)
+                norm_unit(done)
+                rotate_unit(done)
+                add_unit(done)
+                if done % UNITS_PER_GROUP == UNITS_PER_GROUP - 1:
+                    store_group(done // UNITS_PER_GROUP)

@@ -35,6 +35,9 @@ UNITS_PER_GROUP = GROUP // UNIT
 UNITS_PER_CHUNK = BATCH * UNITS_PER_GROUP
 UNITS = GROUPS * UNITS_PER_GROUP
 LOAD_AHEAD = 5
+QUANTISE_LAG = 1
+PROJECT_LAG = 2
+ROTATE_LAG = 3
 
 FLOPS = 2 * BATCH * SEQ * HIDDEN * HEADS * HD
 
@@ -207,15 +210,13 @@ def tile_biboattention_pa_t_kernel(
             first = (u % UNITS_PER_GROUP) * UNIT
             if first == 0:
                 results[n] = out_pool.tile([P, HEADS, GROUP, HD], F32, name="result")
-            for i in range(2):
-                here = slice(i * HALF, (i + 1) * HALF)
-                there = slice((1 - i) * HALF, (2 - i) * HALF)
-                nc.gpsimd.tensor_tensor(
-                    out=results[n][:, :, first : first + UNIT, here],
-                    in0=products[u][:, :, :, 0, here],
-                    in1=products[u][:, :, :, 1, there],
-                    op=ALU.add,
-                )
+            halves = products[u][:].rearrange("p h s a (i d) -> p h s a i d", i=2)
+            nc.gpsimd.tensor_tensor(
+                out=results[n][:, :, first : first + UNIT, :].rearrange("p h s (i d) -> p h s i d", i=2),
+                in0=halves[:, :, :, 0],
+                in1=halves[:, :, :, 1, ::-1],
+                op=ALU.add,
+            )
 
         def store_group(n):
             b = n % BATCH
@@ -282,7 +283,7 @@ def tile_biboattention_pa_t_kernel(
             (slice(Q_HEADS * HD, HEADS * HD), wk_codes, wk_scales, HD),
         )
 
-        for step in range(UNITS + 1):
+        for step in range(UNITS + ROTATE_LAG):
             if step % UNITS_PER_GROUP == 0 and step // UNITS_PER_GROUP + LOAD_AHEAD < GROUPS:
                 load_rows(step // UNITS_PER_GROUP + LOAD_AHEAD)
             if step % UNITS_PER_CHUNK == 0 and step // UNITS_PER_CHUNK + 1 < CHUNKS:
@@ -290,14 +291,16 @@ def tile_biboattention_pa_t_kernel(
             if step < UNITS:
                 transpose_unit(step)
                 copy_unit(step)
-                quantise_unit(step)
+            if 0 <= step - QUANTISE_LAG < UNITS:
+                quantise_unit(step - QUANTISE_LAG)
             following = step + 1
             if following < UNITS and following % UNITS_PER_CHUNK < UNITS_PER_GROUP:
                 build_tables(following // UNITS_PER_CHUNK, following % UNITS_PER_CHUNK)
-            if step >= 1:
-                done = step - 1
-                project_unit(done)
-                norm_unit(done)
+            if 0 <= step - PROJECT_LAG < UNITS:
+                project_unit(step - PROJECT_LAG)
+                norm_unit(step - PROJECT_LAG)
+            if 0 <= step - ROTATE_LAG:
+                done = step - ROTATE_LAG
                 rotate_unit(done)
                 add_unit(done)
                 if done % UNITS_PER_GROUP == UNITS_PER_GROUP - 1:

@@ -34,7 +34,8 @@ GROUPS = CHUNKS * BATCH
 UNITS_PER_GROUP = GROUP // UNIT
 UNITS_PER_CHUNK = BATCH * UNITS_PER_GROUP
 UNITS = GROUPS * UNITS_PER_GROUP
-LOAD_AHEAD = 5
+LOAD_AHEAD = 10
+HEAD_CHUNK = 1
 QUANTISE_LAG = 1
 PROJECT_LAG = 2
 ROTATE_LAG = 3
@@ -64,14 +65,15 @@ def tile_biboattention_pa_t_kernel(
     with ExitStack() as ctx:
         const = ctx.enter_context(tc.tile_pool(name="const", bufs=1))
         x_pool = ctx.enter_context(tc.tile_pool(name="x", bufs=LOAD_AHEAD + 1))
-        angle_pool = ctx.enter_context(tc.tile_pool(name="angle", bufs=2))
+        angle_pool = ctx.enter_context(tc.tile_pool(name="angle", bufs=CHUNKS))
         table_pool = ctx.enter_context(tc.tile_pool(name="table", bufs=2))
         mx_pool = ctx.enter_context(tc.tile_pool(name="mx", bufs=3))
         stat_pool = ctx.enter_context(tc.tile_pool(name="stat", bufs=4))
         prod_pool = ctx.enter_context(tc.tile_pool(name="prod", bufs=3))
         out_pool = ctx.enter_context(tc.tile_pool(name="out", bufs=3))
-        psum_t = ctx.enter_context(tc.psum_pool(name="psum_t", bufs=2 * UNIT))
+        psum_t = ctx.enter_context(tc.psum_pool(name="psum_t", bufs=UNIT))
         psum_o = ctx.enter_context(tc.psum_pool(name="psum_o", bufs=2 * UNIT))
+        psum_w = ctx.enter_context(tc.psum_pool(name="psum_w", bufs=1))
         ctx.enter_context(tc.manual_schedule())
 
         cos_slices = cos.rearrange("(p t) d -> p t d", t=SLICES)
@@ -98,42 +100,42 @@ def tile_biboattention_pa_t_kernel(
             nc.sync.dma_start(out=angle[:, 1], in_=sin_slices[:, group_slices(chunk * BATCH), :])
             angles[chunk] = angle
 
-        def build_tables(chunk, v):
+        def build_tables(engine, for_cos, for_sin, chunk, v):
             if v == 0:
                 tables[chunk] = table_pool.tile([P, GROUP, HEADS, 2, HD], F32, name="table")
             table = tables[chunk]
             angle = angles[chunk]
             mine = slice(v * UNIT, (v + 1) * UNIT)
-            nc.vector.tensor_tensor(
+            engine.tensor_tensor(
                 out=table[:, mine, :, 0, :],
                 in0=angle[:, 0, mine].unsqueeze(2).to_broadcast([P, UNIT, HEADS, HD]),
-                in1=w_cos[:].unsqueeze(1).to_broadcast([P, UNIT, HEADS, HD]),
+                in1=for_cos.unsqueeze(1).to_broadcast([P, UNIT, HEADS, HD]),
                 op=ALU.mult,
             )
             for i in range(2):
                 here = slice(i * HALF, (i + 1) * HALF)
                 there = slice((1 - i) * HALF, (2 - i) * HALF)
-                nc.vector.tensor_tensor(
+                engine.tensor_tensor(
                     out=table[:, mine, :, 1, here],
                     in0=angle[:, 1, mine, there].unsqueeze(2).to_broadcast([P, UNIT, HEADS, HALF]),
-                    in1=w_sin[:, :, here].unsqueeze(1).to_broadcast([P, UNIT, HEADS, HALF]),
+                    in1=for_sin[:, :, here].unsqueeze(1).to_broadcast([P, UNIT, HEADS, HALF]),
                     op=ALU.mult,
                 )
 
-        def load_rows(n):
-            x_rows = x_pool.tile([P, GROUP * HIDDEN], BF16)
+        def load_rows(u):
+            n = u // UNITS_PER_GROUP
+            first = (n // BATCH) * GROUP + (u % UNITS_PER_GROUP) * UNIT
+            x_rows = x_pool.tile([P, UNIT * HIDDEN], BF16)
             nc.sync.dma_start(
-                out=x_rows[:].rearrange("p (t k) -> p t k", t=GROUP),
-                in_=hidden_states[n % BATCH].rearrange("(p t) k -> p t k", t=SLICES)[:, group_slices(n), :],
+                out=x_rows[:].rearrange("p (t k) -> p t k", t=UNIT),
+                in_=hidden_states[n % BATCH].rearrange("(p t) k -> p t k", t=SLICES)[:, first : first + UNIT, :],
             )
-            x_words[n] = x_rows[:].bitcast(F32)
+            x_words[u] = x_rows[:].bitcast(F32)
 
         def transpose_unit(u):
-            words = x_words[u // UNITS_PER_GROUP]
-            first = (u % UNITS_PER_GROUP) * UNIT
             banks[u] = [
-                transpose_rows(nc, psum_t, ident, words[:, t * WORDS : (t + 1) * WORDS])
-                for t in range(first, first + UNIT)
+                transpose_rows(nc, psum_t, ident, x_words[u][:, s * WORDS : (s + 1) * WORDS])
+                for s in range(UNIT)
             ]
 
         def copy_unit(u):
@@ -240,9 +242,13 @@ def tile_biboattention_pa_t_kernel(
         w_raw = const.tile([P, HEADS, HIDDEN], BF16)
         nc.sync.dma_start(out=w_raw[:, 0:Q_HEADS, :], in_=wq.rearrange("(a p) k -> p a k", p=P))
         nc.sync.dma_start(out=w_raw[:, Q_HEADS, :], in_=wk)
+        load_rows(0)
         load_angles(0)
-        for n in range(LOAD_AHEAD):
-            load_rows(n)
+        load_angles(HEAD_CHUNK)
+        for u in range(1, LOAD_AHEAD):
+            load_rows(u)
+        for chunk in range(HEAD_CHUNK + 1, CHUNKS):
+            load_angles(chunk)
 
         ident = const.tile([P, P], F32)
         make_identity(nc, ident[:])
@@ -260,7 +266,8 @@ def tile_biboattention_pa_t_kernel(
         w_sin = const.tile([P, HEADS, HD], F32)
         nc.vector.tensor_copy(out=w_sin[:, :, 0:HALF], in_=w_cos[:, :, 0:HALF])
         nc.vector.tensor_scalar_mul(out=w_sin[:, :, HALF:HD], in0=w_cos[:, :, HALF:HD], scalar1=-1.0)
-        build_tables(0, 0)
+        for v in range(UNITS_PER_GROUP):
+            build_tables(nc.gpsimd, w_cos[:], w_sin[:], HEAD_CHUNK, v)
 
         wq_grouped = const.tile([P, PASSES * Q_HEADS * HD * 4], BF16, align_bytes=64)
         wk_grouped = const.tile([P, PASSES * HD * 4], BF16, align_bytes=64)
@@ -283,19 +290,24 @@ def tile_biboattention_pa_t_kernel(
             (slice(Q_HEADS * HD, HEADS * HD), wk_codes, wk_scales, HD),
         )
 
+        w_cos_psum = psum_w.tile([P, HEADS, HD], F32)
+        w_sin_psum = psum_w.tile([P, HEADS, HD], F32)
+
         for step in range(UNITS + ROTATE_LAG):
-            if step % UNITS_PER_GROUP == 0 and step // UNITS_PER_GROUP + LOAD_AHEAD < GROUPS:
-                load_rows(step // UNITS_PER_GROUP + LOAD_AHEAD)
-            if step % UNITS_PER_CHUNK == 0 and step // UNITS_PER_CHUNK + 1 < CHUNKS:
-                load_angles(step // UNITS_PER_CHUNK + 1)
+            if step + LOAD_AHEAD < UNITS:
+                load_rows(step + LOAD_AHEAD)
             if step < UNITS:
                 transpose_unit(step)
                 copy_unit(step)
+            if step == 0:
+                nc.tensor.matmul(out=w_cos_psum[:], lhsT=ident[:], rhs=w_cos[:], start=True, stop=True)
+                nc.tensor.matmul(out=w_sin_psum[:], lhsT=ident[:], rhs=w_sin[:], start=True, stop=True)
             if 0 <= step - QUANTISE_LAG < UNITS:
-                quantise_unit(step - QUANTISE_LAG)
-            following = step + 1
-            if following < UNITS and following % UNITS_PER_CHUNK < UNITS_PER_GROUP:
-                build_tables(following // UNITS_PER_CHUNK, following % UNITS_PER_CHUNK)
+                fresh = step - QUANTISE_LAG
+                quantise_unit(fresh)
+                chunk, v = divmod(fresh, UNITS_PER_CHUNK)
+                if v < UNITS_PER_GROUP and chunk != HEAD_CHUNK:
+                    build_tables(nc.vector, w_cos_psum[:], w_sin_psum[:], chunk, v)
             if 0 <= step - PROJECT_LAG < UNITS:
                 project_unit(step - PROJECT_LAG)
                 norm_unit(step - PROJECT_LAG)

@@ -36,6 +36,7 @@ UNITS_PER_CHUNK = BATCH * UNITS_PER_GROUP
 UNITS = GROUPS * UNITS_PER_GROUP
 LOAD_AHEAD = 10
 HEAD_CHUNK = 1
+VECTOR_ADDS_EVERY = 8
 QUANTISE_LAG = 1
 PROJECT_LAG = 2
 ROTATE_LAG = 3
@@ -67,9 +68,9 @@ def tile_biboattention_pa_t_kernel(
         x_pool = ctx.enter_context(tc.tile_pool(name="x", bufs=LOAD_AHEAD + 1))
         angle_pool = ctx.enter_context(tc.tile_pool(name="angle", bufs=CHUNKS))
         table_pool = ctx.enter_context(tc.tile_pool(name="table", bufs=2))
-        mx_pool = ctx.enter_context(tc.tile_pool(name="mx", bufs=3))
-        stat_pool = ctx.enter_context(tc.tile_pool(name="stat", bufs=4))
-        prod_pool = ctx.enter_context(tc.tile_pool(name="prod", bufs=3))
+        mx_pool = ctx.enter_context(tc.tile_pool(name="mx", bufs=4))
+        stat_pool = ctx.enter_context(tc.tile_pool(name="stat", bufs=6))
+        prod_pool = ctx.enter_context(tc.tile_pool(name="prod", bufs=4))
         out_pool = ctx.enter_context(tc.tile_pool(name="out", bufs=3))
         psum_t = ctx.enter_context(tc.psum_pool(name="psum_t", bufs=UNIT))
         psum_o = ctx.enter_context(tc.psum_pool(name="psum_o", bufs=2 * UNIT))
@@ -213,7 +214,8 @@ def tile_biboattention_pa_t_kernel(
             if first == 0:
                 results[n] = out_pool.tile([P, HEADS, GROUP, HD], F32, name="result")
             halves = products[u][:].rearrange("p h s a (i d) -> p h s a i d", i=2)
-            nc.gpsimd.tensor_tensor(
+            engine = nc.vector if u % VECTOR_ADDS_EVERY == VECTOR_ADDS_EVERY - 1 else nc.gpsimd
+            engine.tensor_tensor(
                 out=results[n][:, :, first : first + UNIT, :].rearrange("p h s (i d) -> p h s i d", i=2),
                 in0=halves[:, :, :, 0],
                 in1=halves[:, :, :, 1, ::-1],
@@ -296,24 +298,24 @@ def tile_biboattention_pa_t_kernel(
         for step in range(UNITS + ROTATE_LAG):
             if step + LOAD_AHEAD < UNITS:
                 load_rows(step + LOAD_AHEAD)
-            if step < UNITS:
-                transpose_unit(step)
-                copy_unit(step)
-            if step == 0:
-                nc.tensor.matmul(out=w_cos_psum[:], lhsT=ident[:], rhs=w_cos[:], start=True, stop=True)
-                nc.tensor.matmul(out=w_sin_psum[:], lhsT=ident[:], rhs=w_sin[:], start=True, stop=True)
-            if 0 <= step - QUANTISE_LAG < UNITS:
-                fresh = step - QUANTISE_LAG
-                quantise_unit(fresh)
-                chunk, v = divmod(fresh, UNITS_PER_CHUNK)
-                if v < UNITS_PER_GROUP and chunk != HEAD_CHUNK:
-                    build_tables(nc.vector, w_cos_psum[:], w_sin_psum[:], chunk, v)
-            if 0 <= step - PROJECT_LAG < UNITS:
-                project_unit(step - PROJECT_LAG)
-                norm_unit(step - PROJECT_LAG)
             if 0 <= step - ROTATE_LAG:
                 done = step - ROTATE_LAG
                 rotate_unit(done)
                 add_unit(done)
                 if done % UNITS_PER_GROUP == UNITS_PER_GROUP - 1:
                     store_group(done // UNITS_PER_GROUP)
+            if 0 <= step - PROJECT_LAG < UNITS:
+                project_unit(step - PROJECT_LAG)
+                norm_unit(step - PROJECT_LAG)
+            if 0 <= step - QUANTISE_LAG < UNITS:
+                fresh = step - QUANTISE_LAG
+                quantise_unit(fresh)
+                chunk, v = divmod(fresh, UNITS_PER_CHUNK)
+                if v < UNITS_PER_GROUP and chunk != HEAD_CHUNK:
+                    build_tables(nc.vector, w_cos_psum[:], w_sin_psum[:], chunk, v)
+            if step < UNITS:
+                transpose_unit(step)
+                copy_unit(step)
+            if step == 0:
+                nc.tensor.matmul(out=w_cos_psum[:], lhsT=ident[:], rhs=w_cos[:], start=True, stop=True)
+                nc.tensor.matmul(out=w_sin_psum[:], lhsT=ident[:], rhs=w_sin[:], start=True, stop=True)

import math
from contextlib import ExitStack

import concourse.mybir as mybir
from concourse.masks import make_identity

F32 = mybir.dt.float32
BF16 = mybir.dt.bfloat16
U32 = mybir.dt.uint32
U8 = mybir.dt.uint8
FP8X4 = mybir.dt.float8_e4m3fn_x4
ALU = mybir.AluOpType
ACT = mybir.ActivationFunctionType

P = 128
BATCH = 4
SEQ = 2048
HIDDEN = 1024
Q_HEADS = 2
HEADS = 3
HD = 128
HALF = HD // 2
EPS = 1e-6

K_PASS = 4 * P
PASSES = HIDDEN // K_PASS
WORDS = HIDDEN // 2
BLOCKS = WORDS // P
SLICES = SEQ // P
GROUP = 4
UNIT = 2
CHUNKS = SLICES // GROUP
GROUPS = CHUNKS * BATCH
UNITS_PER_GROUP = GROUP // UNIT
UNITS_PER_CHUNK = BATCH * UNITS_PER_GROUP
UNITS = GROUPS * UNITS_PER_GROUP
LOAD_AHEAD = 10
HEAD_CHUNK = 1
VECTOR_ADDS_EVERY = 8
QUANTISE_LAG = 1
PROJECT_LAG = 2
ROTATE_LAG = 3

FLOPS = 2 * BATCH * SEQ * HIDDEN * HEADS * HD


def transpose_rows(nc, psum_t, ident, words):
    bank = psum_t.tile([P, WORDS], F32, name="bank")
    for j in range(BLOCKS):
        cols = slice(j * P, (j + 1) * P)
        nc.tensor.transpose(bank[:, cols], words[:, cols], ident[:])
    return bank


def copy_grouped(nc, bank, grouped_words):
    nc.scalar.copy(
        out=grouped_words,
        in_=bank[:].rearrange("p (g u r) -> p g r u", g=PASSES, u=2),
    )


def tile_biboattention_pa_t_kernel(
    tc, hidden_states, cos, sin, wq, wk, q_norm_w, k_norm_w, ssmax_scale, out_0, out_1
):
    nc = tc.nc
    with ExitStack() as ctx:
        const = ctx.enter_context(tc.tile_pool(name="const", bufs=1))
        x_pool = ctx.enter_context(tc.tile_pool(name="x", bufs=LOAD_AHEAD + 1))
        angle_pool = ctx.enter_context(tc.tile_pool(name="angle", bufs=CHUNKS))
        table_pool = ctx.enter_context(tc.tile_pool(name="table", bufs=2))
        mx_pool = ctx.enter_context(tc.tile_pool(name="mx", bufs=4))
        stat_pool = ctx.enter_context(tc.tile_pool(name="stat", bufs=6))
        prod_pool = ctx.enter_context(tc.tile_pool(name="prod", bufs=4))
        out_pool = ctx.enter_context(tc.tile_pool(name="out", bufs=3))
        psum_t = ctx.enter_context(tc.psum_pool(name="psum_t", bufs=UNIT))
        psum_o = ctx.enter_context(tc.psum_pool(name="psum_o", bufs=2 * UNIT))
        psum_w = ctx.enter_context(tc.psum_pool(name="psum_w", bufs=1))
        ctx.enter_context(tc.manual_schedule())

        cos_slices = cos.rearrange("(p t) d -> p t d", t=SLICES)
        sin_slices = sin.rearrange("(p t) d -> p t d", t=SLICES)

        angles = {}
        tables = {}
        x_words = {}
        banks = {}
        groupeds = {}
        operands = {}
        raws = {}
        rstds = {}
        products = {}
        results = {}

        def group_slices(n):
            chunk = n // BATCH
            return slice(chunk * GROUP, (chunk + 1) * GROUP)

        def load_angles(chunk):
            angle = angle_pool.tile([P, 2, GROUP, HD], BF16)
            nc.sync.dma_start(out=angle[:, 0], in_=cos_slices[:, group_slices(chunk * BATCH), :])
            nc.sync.dma_start(out=angle[:, 1], in_=sin_slices[:, group_slices(chunk * BATCH), :])
            angles[chunk] = angle

        def build_tables(engine, for_cos, for_sin, chunk, v):
            if v == 0:
                tables[chunk] = table_pool.tile([P, GROUP, HEADS, 2, HD], F32, name="table")
            table = tables[chunk]
            angle = angles[chunk]
            mine = slice(v * UNIT, (v + 1) * UNIT)
            engine.tensor_tensor(
                out=table[:, mine, :, 0, :],
                in0=angle[:, 0, mine].unsqueeze(2).to_broadcast([P, UNIT, HEADS, HD]),
                in1=for_cos.unsqueeze(1).to_broadcast([P, UNIT, HEADS, HD]),
                op=ALU.mult,
            )
            for i in range(2):
                here = slice(i * HALF, (i + 1) * HALF)
                there = slice((1 - i) * HALF, (2 - i) * HALF)
                engine.tensor_tensor(
                    out=table[:, mine, :, 1, here],
                    in0=angle[:, 1, mine, there].unsqueeze(2).to_broadcast([P, UNIT, HEADS, HALF]),
                    in1=for_sin[:, :, here].unsqueeze(1).to_broadcast([P, UNIT, HEADS, HALF]),
                    op=ALU.mult,
                )

        def load_rows(u):
            n = u // UNITS_PER_GROUP
            first = (n // BATCH) * GROUP + (u % UNITS_PER_GROUP) * UNIT
            x_rows = x_pool.tile([P, UNIT * HIDDEN], BF16)
            nc.sync.dma_start(
                out=x_rows[:].rearrange("p (t k) -> p t k", t=UNIT),
                in_=hidden_states[n % BATCH].rearrange("(p t) k -> p t k", t=SLICES)[:, first : first + UNIT, :],
            )
            x_words[u] = x_rows[:].bitcast(F32)

        def transpose_unit(u):
            banks[u] = [
                transpose_rows(nc, psum_t, ident, x_words[u][:, s * WORDS : (s + 1) * WORDS])
                for s in range(UNIT)
            ]

        def copy_unit(u):
            grouped = mx_pool.tile([P, UNIT * HIDDEN], BF16, align_bytes=64)
            grouped_words = grouped[:].bitcast(F32).rearrange(
                "p (s g r u) -> p s g r u", s=UNIT, g=PASSES, u=2
            )
            for s in range(UNIT):
                copy_grouped(nc, banks[u][s], grouped_words[:, s])
            groupeds[u] = grouped

        def quantise_unit(u):
            codes = mx_pool.tile([P, UNIT * PASSES * P], U32, align_bytes=64)
            scales = mx_pool.tile([P, UNIT * PASSES * P], U8, align_bytes=64)
            nc.vector.quantize_mx(out=codes[:].bitcast(FP8X4), scales=scales[:], in_=groupeds[u][:])
            operands[u] = (codes, scales)

        def project_unit(u):
            codes, scales = operands[u]
            raws[u] = []
            for s in range(UNIT):
                raw = psum_o.tile([P, HEADS * HD], F32)
                for cols, w_codes, w_scales, width in projections:
                    for g in range(PASSES):
                        tokens = slice((s * PASSES + g) * P, (s * PASSES + g + 1) * P)
                        features = slice(g * width, (g + 1) * width)
                        nc.tensor.matmul_mx(
                            out=raw[:, cols],
                            lhsT=codes[:, tokens].bitcast(FP8X4),
                            lhsT_scale=scales[:, tokens],
                            rhs=w_codes[:, features].bitcast(FP8X4),
                            rhs_scale=w_scales[:, features],
                            start=(g == 0),
                            stop=(g == PASSES - 1),
                        )
                raws[u].append(raw)

        def norm_unit(u):
            sumsq = stat_pool.tile([P, UNIT * HEADS], F32)
            for s in range(UNIT):
                squares = stat_pool.tile([P, HEADS * HD], BF16)
                for h in range(HEADS):
                    head = slice(h * HD, (h + 1) * HD)
                    nc.scalar.activation(
                        out=squares[:, head],
                        in_=raws[u][s][:, head],
                        func=ACT.Square,
                        accum_out=sumsq[:, s * HEADS + h : s * HEADS + h + 1],
                    )
            rstd = stat_pool.tile([P, UNIT * HEADS], F32)
            nc.scalar.activation(
                out=rstd[:], in_=sumsq[:], func=ACT.Abs_reciprocal_sqrt, bias=eps[:], scale=1.0 / HD
            )
            rstds[u] = rstd

        def rotate_unit(u):
            table = tables[u // UNITS_PER_CHUNK]
            first = (u % UNITS_PER_GROUP) * UNIT
            product = prod_pool.tile([P, HEADS, UNIT, 2, HD], F32)
            for s in range(UNIT):
                for h in range(HEADS):
                    nc.vector.scalar_tensor_tensor(
                        out=product[:, h, s],
                        in0=raws[u][s][:, h * HD : (h + 1) * HD].unsqueeze(1).to_broadcast([P, 2, HD]),
                        scalar=rstds[u][:, s * HEADS + h : s * HEADS + h + 1],
                        in1=table[:, first + s, h],
                        op0=ALU.mult,
                        op1=ALU.mult,
                    )
            products[u] = product

        def add_unit(u):
            n = u // UNITS_PER_GROUP
            first = (u % UNITS_PER_GROUP) * UNIT
            if first == 0:
                results[n] = out_pool.tile([P, HEADS, GROUP, HD], F32, name="result")
            halves = products[u][:].rearrange("p h s a (i d) -> p h s a i d", i=2)
            engine = nc.vector if u % VECTOR_ADDS_EVERY == VECTOR_ADDS_EVERY - 1 else nc.gpsimd
            engine.tensor_tensor(
                out=results[n][:, :, first : first + UNIT, :].rearrange("p h s (i d) -> p h s i d", i=2),
                in0=halves[:, :, :, 0],
                in1=halves[:, :, :, 1, ::-1],
                op=ALU.add,
            )

        def store_group(n):
            b = n % BATCH
            nc.sync.dma_start(
                out=out_0[b].rearrange("h (p t) d -> p h t d", t=SLICES)[:, :, group_slices(n), :],
                in_=results[n][:, 0:Q_HEADS],
            )
            nc.sync.dma_start(
                out=out_1[b, 0].rearrange("(p t) d -> p t d", t=SLICES)[:, group_slices(n), :],
                in_=results[n][:, Q_HEADS],
            )

        wq_rows = const.tile([P, HD], BF16)
        wk_rows = const.tile([P, HD], BF16)
        gain_rows = const.tile([P, Q_HEADS], BF16)
        nc.scalar.dma_start(out=wq_rows[:], in_=q_norm_w.partition_broadcast(P))
        nc.scalar.dma_start(out=wk_rows[:], in_=k_norm_w.partition_broadcast(P))
        nc.scalar.dma_start(
            out=gain_rows[:], in_=ssmax_scale.rearrange("a h b c -> (a h b c)").partition_broadcast(P)
        )
        w_raw = const.tile([P, HEADS, HIDDEN], BF16)
        nc.sync.dma_start(out=w_raw[:, 0:Q_HEADS, :], in_=wq.rearrange("(a p) k -> p a k", p=P))
        nc.sync.dma_start(out=w_raw[:, Q_HEADS, :], in_=wk)
        load_rows(0)
        load_angles(0)
        load_angles(HEAD_CHUNK)
        for u in range(1, LOAD_AHEAD):
            load_rows(u)
        for chunk in range(HEAD_CHUNK + 1, CHUNKS):
            load_angles(chunk)

        ident = const.tile([P, P], F32)
        make_identity(nc, ident[:])
        eps = const.tile([P, 1], F32)
        nc.vector.memset(eps[:], EPS)
        warm = const.tile([P, 1], F32)
        nc.scalar.activation(out=warm[:], in_=eps[:], func=ACT.Abs_reciprocal_sqrt)

        gain = const.tile([P, Q_HEADS], F32)
        nc.vector.tensor_scalar_mul(out=gain[:], in0=gain_rows[:], scalar1=math.log(SEQ))
        w_cos = const.tile([P, HEADS, HD], F32)
        for h in range(Q_HEADS):
            nc.vector.tensor_scalar_mul(out=w_cos[:, h, :], in0=wq_rows[:], scalar1=gain[:, h : h + 1])
        nc.vector.tensor_copy(out=w_cos[:, Q_HEADS, :], in_=wk_rows[:])
        w_sin = const.tile([P, HEADS, HD], F32)
        nc.vector.tensor_copy(out=w_sin[:, :, 0:HALF], in_=w_cos[:, :, 0:HALF])
        nc.vector.tensor_scalar_mul(out=w_sin[:, :, HALF:HD], in0=w_cos[:, :, HALF:HD], scalar1=-1.0)
        for v in range(UNITS_PER_GROUP):
            build_tables(nc.gpsimd, w_cos[:], w_sin[:], HEAD_CHUNK, v)

        wq_grouped = const.tile([P, PASSES * Q_HEADS * HD * 4], BF16, align_bytes=64)
        wk_grouped = const.tile([P, PASSES * HD * 4], BF16, align_bytes=64)
        wq_words = wq_grouped[:].bitcast(F32).rearrange("p (g n u) -> p g n u", g=PASSES, u=2)
        wk_words = wk_grouped[:].bitcast(F32).rearrange("p (g n u) -> p g n u", g=PASSES, u=2)
        for h in range(HEADS):
            bank = transpose_rows(nc, psum_t, ident, w_raw[:, h, :].bitcast(F32))
            if h < Q_HEADS:
                copy_grouped(nc, bank, wq_words[:, :, h * HD : (h + 1) * HD, :])
            else:
                copy_grouped(nc, bank, wk_words)
        wq_codes = const.tile([P, PASSES * Q_HEADS * HD], U32, align_bytes=64)
        wq_scales = const.tile([P, PASSES * Q_HEADS * HD], U8, align_bytes=64)
        wk_codes = const.tile([P, PASSES * HD], U32, align_bytes=64)
        wk_scales = const.tile([P, PASSES * HD], U8, align_bytes=64)
        nc.vector.quantize_mx(out=wq_codes[:].bitcast(FP8X4), scales=wq_scales[:], in_=wq_grouped[:])
        nc.vector.quantize_mx(out=wk_codes[:].bitcast(FP8X4), scales=wk_scales[:], in_=wk_grouped[:])
        projections = (
            (slice(0, Q_HEADS * HD), wq_codes, wq_scales, Q_HEADS * HD),
            (slice(Q_HEADS * HD, HEADS * HD), wk_codes, wk_scales, HD),
        )

        w_cos_psum = psum_w.tile([P, HEADS, HD], F32)
        w_sin_psum = psum_w.tile([P, HEADS, HD], F32)

        for step in range(UNITS + ROTATE_LAG):
            if step + LOAD_AHEAD < UNITS:
                load_rows(step + LOAD_AHEAD)
            if 0 <= step - ROTATE_LAG:
                done = step - ROTATE_LAG
                rotate_unit(done)
                add_unit(done)
                if done % UNITS_PER_GROUP == UNITS_PER_GROUP - 1:
                    store_group(done // UNITS_PER_GROUP)
            if 0 <= step - PROJECT_LAG < UNITS:
                project_unit(step - PROJECT_LAG)
                norm_unit(step - PROJECT_LAG)
            if 0 <= step - QUANTISE_LAG < UNITS:
                fresh = step - QUANTISE_LAG
                quantise_unit(fresh)
                chunk, v = divmod(fresh, UNITS_PER_CHUNK)
                if v < UNITS_PER_GROUP and chunk != HEAD_CHUNK:
                    build_tables(nc.vector, w_cos_psum[:], w_sin_psum[:], chunk, v)
            if step < UNITS:
                transpose_unit(step)
                copy_unit(step)
            if step == 0:
                nc.tensor.matmul(out=w_cos_psum[:], lhsT=ident[:], rhs=w_cos[:], start=True, stop=True)
                nc.tensor.matmul(out=w_sin_psum[:], lhsT=ident[:], rhs=w_sin[:], start=True, stop=True)
